import numpy as np
import ml_dtypes


def mxq(x, axis, fmt="e4m3"):
    dtype, down = {"e4m3": (ml_dtypes.float8_e4m3fn, 7), "e5m2": (ml_dtypes.float8_e5m2, 14)}[fmt]
    v = np.moveaxis(np.asarray(x, np.float32).astype(ml_dtypes.bfloat16).astype(np.float64), axis, -1)
    blocks = v.reshape(v.shape[:-1] + (-1, 32))
    amax = np.abs(blocks).max(-1, keepdims=True)
    byte = np.maximum(np.where(amax > 0, np.frexp(amax)[1] - 1 + 127, 0) - down, 1)
    scale = np.exp2(byte - 127.0)
    codes = (blocks / scale).astype(np.float32).astype(dtype).astype(np.float64)
    return np.moveaxis((codes * scale).reshape(v.shape), -1, axis)


WIDE = False


def mx_kscale(k):
    if not WIDE:
        return np.ones(k)
    levels = np.array([10, -10, 5, -5, 0])
    a = np.random.permutation(np.resize(levels, k // 512 * 4)).reshape(k // 512, 4)
    idx = np.arange(k)
    return np.exp2(a[idx // 512, idx % 128 // 32])


BF16 = ml_dtypes.bfloat16


def bf(x):
    return np.asarray(x, np.float32).astype(BF16)


def f64(x):
    return np.asarray(x).astype(np.float64)


B, N, F, DIM, H, DH, D3 = 2, 4, 16, 512, 8, 64, 512
W = H * D3
SCALE = 1.0 / (np.sqrt(DH) * H)
QS = np.sqrt(1.5 / (SCALE * np.sqrt(D3)))


def setup_inputs():
    s, t = mx_kscale(DIM), mx_kscale(D3)
    th = np.tile(t, H)
    return {"x": bf(np.random.standard_normal((B, N * F, DIM)) * s),
            "Wq": bf(np.random.standard_normal((DIM, W)) * QS / np.sqrt(DIM) / s[:, None] * th),
            "bq": bf(np.random.standard_normal(W) * 0.2 * QS * th),
            "k": bf(np.random.standard_normal((B, H, N, F, D3)) * QS / t)}


def reference(x, Wq, bq, k):
    y = (mxq(f64(x), 2, "e4m3") @ mxq(f64(Wq), 0, "e4m3")) + f64(bq)
    q = y.reshape(B, F, N, H, D3).transpose(0, 3, 2, 1, 4)
    s = (mxq(q, 4, "e4m3") @ mxq(f64(k), 4, "e4m3").transpose(0, 1, 2, 4, 3)) * SCALE
    e = np.exp(s - s.max(-1, keepdims=True))
    return e / e.sum(-1, keepdims=True)

@@ -1,0 +1,240 @@
+from contextlib import ExitStack
+
+import concourse.mybir as mybir
+from concourse.masks import make_identity
+
+FP8X4 = mybir.dt.float8_e4m3fn_x4
+BF16 = mybir.dt.bfloat16
+F32 = mybir.dt.float32
+U32 = mybir.dt.uint32
+U8 = mybir.dt.uint8
+ALU = mybir.AluOpType
+ACT = mybir.ActivationFunctionType
+AXIS = mybir.AxisListType
+
+P = 128
+QUADRANT = 32
+PACK = 4
+PAIR = 2
+CLIPS, PATCHES, FRAMES, HEADS = 2, 4, 16, 8
+DIM = 512
+FEATURES = 512
+TOKENS = CLIPS * PATCHES * FRAMES
+GROUPS = CLIPS * PATCHES
+HALF_HEADS = HEADS // 2
+SOFTMAX_SCALE = 1.0 / 64.0
+
+VECTOR_COLUMNS = 40
+WEIGHTS_BEFORE_KEYS = 6
+KEYS_ROUND = 5
+
+FLOPS = 2 * TOKENS * DIM * HEADS * FEATURES + 2 * GROUPS * HEADS * FRAMES * FRAMES * FEATURES
+
+
+def tile_dividedspacetimeattention_pa_s_kernel(tc, x, Wq, bq, k, out):
+    nc = tc.nc
+    with ExitStack() as ctx:
+        ctx.enter_context(tc.manual_schedule())
+        keep = ctx.enter_context(tc.tile_pool(name="keep", bufs=1))
+        stage = ctx.enter_context(tc.tile_pool(name="stage", bufs=3))
+        psum_y = ctx.enter_context(tc.psum_pool(name="psum_y", bufs=2))
+        psum_k = ctx.enter_context(tc.psum_pool(name="psum_k", bufs=4))
+        psum_s = ctx.enter_context(tc.psum_pool(name="psum_s", bufs=2))
+
+        x_rows = keep.tile([P, DIM], BF16)
+        nc.sync.dma_start(out=x_rows[:], in_=x.rearrange("b t c -> (b t) c"))
+        bias = keep.tile([P, HEADS, PACK], BF16)
+        nc.sync.dma_start(out=bias[:], in_=bq.rearrange("(h m i) -> m h i", h=HEADS, i=PACK))
+        w_rows = [keep.tile([P, PACK, FEATURES], BF16, name="w_rows%d" % h) for h in range(HEADS)]
+        k_rows = [keep.tile([P, HEADS // 2, FEATURES], BF16, name="k_rows%d" % b) for b in range(CLIPS)]
+        for h in range(HEADS):
+            if h == WEIGHTS_BEFORE_KEYS:
+                for b in range(CLIPS):
+                    nc.sync.dma_start(
+                        out=k_rows[b][:],
+                        in_=k[b].rearrange("h n g d -> (h n g) d").rearrange("(s p) d -> p s d", p=P),
+                    )
+            nc.sync.dma_start(
+                out=w_rows[h][:],
+                in_=Wq[:, h * FEATURES : (h + 1) * FEATURES].rearrange("(p j) w -> p j w", j=PACK),
+            )
+
+        warm = keep.tile([P, 1], F32)
+        nc.vector.memset(warm[:], 0.0)
+        nc.scalar.activation(out=warm[:], in_=warm[:], func=ACT.Exp)
+
+        ident = keep.tile([P, P], F32)
+        make_identity(nc, ident[:])
+        parity = keep.tile([P, 2], F32)
+        nc.vector.tensor_reduce(
+            out=parity[:],
+            in_=ident[:].rearrange("p (q e f) -> p e q f", e=2, f=FRAMES),
+            axis=AXIS.XY,
+            op=ALU.add,
+        )
+
+        def transpose_words(dst, rows, u):
+            words = rows.bitcast(F32).rearrange("r (p u) -> r p u", u=PAIR)
+            nc.tensor.transpose(dst, words[:, :, u], ident[:])
+
+        x_t = psum_s.tile([P, PAIR, TOKENS], F32, tag="s")
+        for u in range(PAIR):
+            transpose_words(x_t[:, u, :], x_rows[:], u)
+        x_grouped = keep.tile([P, TOKENS * PACK], BF16, align_bytes=64)
+        x_grouped_words = x_grouped[:].bitcast(F32).rearrange(
+            "p (b n f u) -> p b n f u", b=CLIPS, n=PATCHES, f=FRAMES
+        )
+        x_t_words = x_t[:].rearrange("p u (b f n) -> p b n f u", b=CLIPS, f=FRAMES)
+        for b in range(CLIPS):
+            nc.vector.tensor_copy(out=x_grouped_words[:, b], in_=x_t_words[:, b])
+        x_codes = keep.tile([P, TOKENS], U32, align_bytes=64)
+        x_scales = keep.tile([P, TOKENS], U8, align_bytes=64)
+        nc.vector.quantize_mx(out=x_codes[:].bitcast(FP8X4), scales=x_scales[:], in_=x_grouped[:])
+
+        w_codes = keep.tile([P, HEADS, FEATURES], U32, align_bytes=64)
+        w_scales = keep.tile([P, HEADS, FEATURES], U8, align_bytes=64)
+        q_codes = keep.tile([P, HEADS, TOKENS], U32, align_bytes=64)
+        q_scales = keep.tile([P, HEADS, TOKENS], U8, align_bytes=64)
+        w_grouped, y_t, q_grouped = {}, {}, {}
+
+        def regroup(h):
+            w_grouped[h] = stage.tile(
+                [P, FEATURES * PACK], BF16, align_bytes=64, tag="w_grouped", name="w_grouped%d" % h
+            )
+            dst = w_grouped[h][:].rearrange("p (i m j) -> p m j i", i=PACK, j=PACK)
+            src = w_rows[h][:].rearrange("p j (m i) -> p m j i", i=PACK)
+            nc.vector.tensor_copy(out=dst[:, :VECTOR_COLUMNS], in_=src[:, :VECTOR_COLUMNS])
+            nc.scalar.copy(out=dst[:, VECTOR_COLUMNS:], in_=src[:, VECTOR_COLUMNS:])
+
+        def project(h):
+            nc.vector.quantize_mx(
+                out=w_codes[:, h, :].bitcast(FP8X4), scales=w_scales[:, h, :], in_=w_grouped[h][:]
+            )
+            y_t[h] = psum_y.tile([P, PACK, TOKENS], F32, tag="y_t", name="y_t%d" % h)
+            for i in range(PACK):
+                quarter = slice(i * P, (i + 1) * P)
+                nc.tensor.matmul_mx(
+                    out=y_t[h][:, i, :],
+                    lhsT=w_codes[:, h, quarter].bitcast(FP8X4),
+                    lhsT_scale=w_scales[:, h, quarter],
+                    rhs=x_codes[:].bitcast(FP8X4),
+                    rhs_scale=x_scales[:],
+                    start=True,
+                    stop=True,
+                )
+
+        def add_bias(h):
+            q_grouped[h] = stage.tile(
+                [P, TOKENS, PACK], BF16, align_bytes=64, tag="q_grouped", name="q_grouped%d" % h
+            )
+            nc.vector.tensor_tensor(
+                out=q_grouped[h][:],
+                in0=y_t[h][:].rearrange("p i t -> p t i"),
+                in1=bias[:, h, :].unsqueeze(1).to_broadcast([P, TOKENS, PACK]),
+                op=ALU.add,
+            )
+
+        def quantise_q(h):
+            nc.vector.quantize_mx(
+                out=q_codes[:, h, :].bitcast(FP8X4),
+                scales=q_scales[:, h, :],
+                in_=q_grouped[h][:].rearrange("p t i -> p (t i)"),
+            )
+
+        k_grouped = keep.tile([P, HEADS * TOKENS * PACK], BF16, align_bytes=64)
+        k_grouped_words = k_grouped[:].bitcast(F32).rearrange(
+            "p (h b c u) -> p h b c u", h=HEADS, b=CLIPS, u=PAIR
+        )
+        k_codes = keep.tile([P, HEADS, TOKENS], U32, align_bytes=64)
+        k_scales = keep.tile([P, HEADS, TOKENS], U8, align_bytes=64)
+        k_t = {}
+
+        def transpose_keys(half):
+            for b in range(CLIPS):
+                k_t[half, b] = psum_k.tile([P, PAIR, 2 * P], F32, tag="k_t", name="k_t%d%d" % (half, b))
+                for s in range(2):
+                    for u in range(PAIR):
+                        transpose_words(
+                            k_t[half, b][:, u, s * P : (s + 1) * P], k_rows[b][:, half * 2 + s, :], u
+                        )
+
+        def quantise_keys(half):
+            heads = slice(half * HALF_HEADS, (half + 1) * HALF_HEADS)
+            for b in range(CLIPS):
+                nc.scalar.copy(
+                    out=k_grouped_words[:, heads, b],
+                    in_=k_t[half, b][:].rearrange("p u (h c) -> p h c u", h=HALF_HEADS),
+                )
+            columns = HALF_HEADS * TOKENS * PACK
+            nc.vector.quantize_mx(
+                out=k_codes[:, heads, :].rearrange("p h c -> p (h c)").bitcast(FP8X4),
+                scales=k_scales[:, heads, :].rearrange("p h c -> p (h c)"),
+                in_=k_grouped[:, half * columns : (half + 1) * columns],
+            )
+
+        regroup(0)
+        for r in range(HEADS + 1):
+            if r < HEADS:
+                project(r)
+            if r >= 1:
+                add_bias(r - 1)
+            if r + 1 < HEADS:
+                regroup(r + 1)
+            else:
+                quantise_keys(r + 1 - HEADS)
+            if r >= 1:
+                quantise_q(r - 1)
+            if 0 <= r - KEYS_ROUND < 2:
+                transpose_keys(r - KEYS_ROUND)
+
+        s_all = []
+        for half in range(2):
+            s_all.append(psum_s.tile([P, HALF_HEADS, GROUPS, FRAMES], F32, tag="s", name="s_all%d" % half))
+            for hh in range(HALF_HEADS):
+                h = half * HALF_HEADS + hh
+                nc.tensor.matmul_mx(
+                    out=s_all[half][:, hh].rearrange("p j g -> p (j g)"),
+                    lhsT=q_codes[:, h, :].bitcast(FP8X4),
+                    lhsT_scale=q_scales[:, h, :],
+                    rhs=k_codes[:, h, :].bitcast(FP8X4),
+                    rhs_scale=k_scales[:, h, :],
+                    start=True,
+                    stop=True,
+                )
+        near = keep.tile([P, HEADS, 2, FRAMES], F32)
+        for half in range(2):
+            heads = slice(half * HALF_HEADS, (half + 1) * HALF_HEADS)
+            for c in range(P // QUADRANT):
+                rows = slice(c * QUADRANT, (c + 1) * QUADRANT)
+                leave = nc.scalar.copy if c < 2 else nc.vector.tensor_copy
+                leave(out=near[rows, heads], in_=s_all[half][rows, :, 2 * c : 2 * c + 2, :])
+        by_head = [P, HEADS, FRAMES]
+        second = keep.tile(by_head, F32)
+        nc.vector.tensor_scalar(
+            out=second[:], in0=near[:, :, 1, :], scalar1=parity[:, 1:2], scalar2=None, op0=ALU.mult
+        )
+        scores = keep.tile(by_head, F32)
+        nc.vector.scalar_tensor_tensor(
+            out=scores[:], in0=near[:, :, 0, :], scalar=parity[:, 0:1], in1=second[:], op0=ALU.mult, op1=ALU.add
+        )
+
+        top = keep.tile([P, HEADS], F32)
+        nc.vector.tensor_reduce(out=top[:], in_=scores[:], axis=AXIS.X, op=ALU.max)
+        shifted = keep.tile(by_head, F32)
+        nc.vector.tensor_tensor(
+            out=shifted[:], in0=scores[:], in1=top[:].unsqueeze(2).to_broadcast(by_head), op=ALU.subtract
+        )
+        weights = keep.tile(by_head, F32)
+        nc.scalar.activation(out=weights[:], in_=shifted[:], func=ACT.Exp, scale=SOFTMAX_SCALE)
+        total = keep.tile([P, HEADS], F32)
+        nc.vector.tensor_reduce(out=total[:], in_=weights[:], axis=AXIS.X, op=ALU.add)
+        inverse = keep.tile([P, HEADS], F32)
+        nc.vector.reciprocal(out=inverse[:], in_=total[:])
+        result = keep.tile(by_head, F32)
+        nc.vector.tensor_tensor(
+            out=result[:], in0=weights[:], in1=inverse[:].unsqueeze(2).to_broadcast(by_head), op=ALU.mult
+        )
+
+        half_p = P // CLIPS
+        nc.sync.dma_start(out=out[0].rearrange("h n f g -> (n f) h g"), in_=result[:half_p])
+        nc.scalar.dma_start(out=out[1].rearrange("h n f g -> (n f) h g"), in_=result[half_p:])

@@ -25,7 +25,6 @@ HALF_HEADS = HEADS // 2
 SOFTMAX_SCALE = 1.0 / 64.0
 
 VECTOR_COLUMNS = 40
-WEIGHTS_BEFORE_KEYS = 6
 KEYS_ROUND = 5
 
 FLOPS = 2 * TOKENS * DIM * HEADS * FEATURES + 2 * GROUPS * HEADS * FRAMES * FRAMES * FEATURES
@@ -41,22 +40,26 @@ def tile_dividedspacetimeattention_pa_s_kernel(tc, x, Wq, bq, k, out):
         psum_k = ctx.enter_context(tc.psum_pool(name="psum_k", bufs=4))
         psum_s = ctx.enter_context(tc.psum_pool(name="psum_s", bufs=2))
 
-        x_rows = keep.tile([P, DIM], BF16)
-        nc.sync.dma_start(out=x_rows[:], in_=x.rearrange("b t c -> (b t) c"))
-        bias = keep.tile([P, HEADS, PACK], BF16)
-        nc.sync.dma_start(out=bias[:], in_=bq.rearrange("(h m i) -> m h i", h=HEADS, i=PACK))
         w_rows = [keep.tile([P, PACK, FEATURES], BF16, name="w_rows%d" % h) for h in range(HEADS)]
-        k_rows = [keep.tile([P, HEADS // 2, FEATURES], BF16, name="k_rows%d" % b) for b in range(CLIPS)]
-        for h in range(HEADS):
-            if h == WEIGHTS_BEFORE_KEYS:
-                for b in range(CLIPS):
-                    nc.sync.dma_start(
-                        out=k_rows[b][:],
-                        in_=k[b].rearrange("h n g d -> (h n g) d").rearrange("(s p) d -> p s d", p=P),
-                    )
+
+        def load_weights(h):
             nc.sync.dma_start(
                 out=w_rows[h][:],
                 in_=Wq[:, h * FEATURES : (h + 1) * FEATURES].rearrange("(p j) w -> p j w", j=PACK),
+            )
+
+        load_weights(0)
+        x_rows = keep.tile([P, DIM], BF16)
+        nc.sync.dma_start(out=x_rows[:], in_=x.rearrange("b t c -> (b t) c"))
+        load_weights(1)
+        bias = keep.tile([P, HEADS, PACK], BF16)
+        nc.sync.dma_start(out=bias[:], in_=bq.rearrange("(h m i) -> m h i", h=HEADS, i=PACK))
+        for h in range(2, HEADS):
+            load_weights(h)
+        k_rows = [keep.tile([P, HEADS // 2, FEATURES], BF16, name="k_rows%d" % b) for b in range(CLIPS)]
+        for b in range(CLIPS):
+            nc.sync.dma_start(
+                out=k_rows[b][:], in_=k[b].rearrange("h n g d -> (h n g) d").rearrange("(s p) d -> p s d", p=P)
             )
 
         warm = keep.tile([P, 1], F32)
@@ -77,19 +80,21 @@ def tile_dividedspacetimeattention_pa_s_kernel(tc, x, Wq, bq, k, out):
             words = rows.bitcast(F32).rearrange("r (p u) -> r p u", u=PAIR)
             nc.tensor.transpose(dst, words[:, :, u], ident[:])
 
-        x_t = psum_s.tile([P, PAIR, TOKENS], F32, tag="s")
-        for u in range(PAIR):
-            transpose_words(x_t[:, u, :], x_rows[:], u)
-        x_grouped = keep.tile([P, TOKENS * PACK], BF16, align_bytes=64)
-        x_grouped_words = x_grouped[:].bitcast(F32).rearrange(
-            "p (b n f u) -> p b n f u", b=CLIPS, n=PATCHES, f=FRAMES
-        )
-        x_t_words = x_t[:].rearrange("p u (b f n) -> p b n f u", b=CLIPS, f=FRAMES)
-        for b in range(CLIPS):
-            nc.vector.tensor_copy(out=x_grouped_words[:, b], in_=x_t_words[:, b])
         x_codes = keep.tile([P, TOKENS], U32, align_bytes=64)
         x_scales = keep.tile([P, TOKENS], U8, align_bytes=64)
-        nc.vector.quantize_mx(out=x_codes[:].bitcast(FP8X4), scales=x_scales[:], in_=x_grouped[:])
+
+        def quantise_x():
+            x_t = psum_s.tile([P, PAIR, TOKENS], F32, tag="s")
+            for u in range(PAIR):
+                transpose_words(x_t[:, u, :], x_rows[:], u)
+            x_grouped = keep.tile([P, TOKENS * PACK], BF16, align_bytes=64)
+            x_grouped_words = x_grouped[:].bitcast(F32).rearrange(
+                "p (b n f u) -> p b n f u", b=CLIPS, n=PATCHES, f=FRAMES
+            )
+            x_t_words = x_t[:].rearrange("p u (b f n) -> p b n f u", b=CLIPS, f=FRAMES)
+            for b in range(CLIPS):
+                nc.vector.tensor_copy(out=x_grouped_words[:, b], in_=x_t_words[:, b])
+            nc.vector.quantize_mx(out=x_codes[:].bitcast(FP8X4), scales=x_scales[:], in_=x_grouped[:])
 
         w_codes = keep.tile([P, HEADS, FEATURES], U32, align_bytes=64)
         w_scales = keep.tile([P, HEADS, FEATURES], U8, align_bytes=64)
@@ -149,8 +154,8 @@ def tile_dividedspacetimeattention_pa_s_kernel(tc, x, Wq, bq, k, out):
         k_scales = keep.tile([P, HEADS, TOKENS], U8, align_bytes=64)
         k_t = {}
 
-        def transpose_keys(half):
-            for b in range(CLIPS):
+        def transpose_keys(b):
+            for half in range(2):
                 k_t[half, b] = psum_k.tile([P, PAIR, 2 * P], F32, tag="k_t", name="k_t%d%d" % (half, b))
                 for s in range(2):
                     for u in range(PAIR):
@@ -173,6 +178,7 @@ def tile_dividedspacetimeattention_pa_s_kernel(tc, x, Wq, bq, k, out):
             )
 
         regroup(0)
+        quantise_x()
         for r in range(HEADS + 1):
             if r < HEADS:
                 project(r)
@@ -201,40 +207,68 @@ def tile_dividedspacetimeattention_pa_s_kernel(tc, x, Wq, bq, k, out):
                     start=True,
                     stop=True,
                 )
-        near = keep.tile([P, HEADS, 2, FRAMES], F32)
-        for half in range(2):
-            heads = slice(half * HALF_HEADS, (half + 1) * HALF_HEADS)
+        halves = range(2)
+        by_head = [P, HALF_HEADS, FRAMES]
+
+        def tiles(shape, name):
+            return [keep.tile(shape, F32, name="%s%d" % (name, half)) for half in halves]
+
+        near = tiles([P, HALF_HEADS, 2, FRAMES], "near")
+        for half in halves:
             for c in range(P // QUADRANT):
                 rows = slice(c * QUADRANT, (c + 1) * QUADRANT)
                 leave = nc.scalar.copy if c < 2 else nc.vector.tensor_copy
-                leave(out=near[rows, heads], in_=s_all[half][rows, :, 2 * c : 2 * c + 2, :])
-        by_head = [P, HEADS, FRAMES]
-        second = keep.tile(by_head, F32)
-        nc.vector.tensor_scalar(
-            out=second[:], in0=near[:, :, 1, :], scalar1=parity[:, 1:2], scalar2=None, op0=ALU.mult
-        )
-        scores = keep.tile(by_head, F32)
-        nc.vector.scalar_tensor_tensor(
-            out=scores[:], in0=near[:, :, 0, :], scalar=parity[:, 0:1], in1=second[:], op0=ALU.mult, op1=ALU.add
-        )
+                leave(out=near[half][rows], in_=s_all[half][rows, :, 2 * c : 2 * c + 2, :])
+        second = tiles(by_head, "second")
+        for half in halves:
+            nc.vector.tensor_scalar(
+                out=second[half][:], in0=near[half][:, :, 1, :], scalar1=parity[:, 1:2], scalar2=None, op0=ALU.mult
+            )
+        scores = tiles(by_head, "scores")
+        for half in halves:
+            nc.vector.scalar_tensor_tensor(
+                out=scores[half][:],
+                in0=near[half][:, :, 0, :],
+                scalar=parity[:, 0:1],
+                in1=second[half][:],
+                op0=ALU.mult,
+                op1=ALU.add,
+            )
 
-        top = keep.tile([P, HEADS], F32)
-        nc.vector.tensor_reduce(out=top[:], in_=scores[:], axis=AXIS.X, op=ALU.max)
-        shifted = keep.tile(by_head, F32)
-        nc.vector.tensor_tensor(
-            out=shifted[:], in0=scores[:], in1=top[:].unsqueeze(2).to_broadcast(by_head), op=ALU.subtract
-        )
-        weights = keep.tile(by_head, F32)
-        nc.scalar.activation(out=weights[:], in_=shifted[:], func=ACT.Exp, scale=SOFTMAX_SCALE)
-        total = keep.tile([P, HEADS], F32)
-        nc.vector.tensor_reduce(out=total[:], in_=weights[:], axis=AXIS.X, op=ALU.add)
-        inverse = keep.tile([P, HEADS], F32)
-        nc.vector.reciprocal(out=inverse[:], in_=total[:])
-        result = keep.tile(by_head, F32)
-        nc.vector.tensor_tensor(
-            out=result[:], in0=weights[:], in1=inverse[:].unsqueeze(2).to_broadcast(by_head), op=ALU.mult
-        )
+        top = tiles([P, HALF_HEADS], "top")
+        for half in halves:
+            nc.vector.tensor_reduce(out=top[half][:], in_=scores[half][:], axis=AXIS.X, op=ALU.max)
+        shifted = tiles(by_head, "shifted")
+        for half in halves:
+            nc.vector.tensor_tensor(
+                out=shifted[half][:],
+                in0=scores[half][:],
+                in1=top[half][:].unsqueeze(2).to_broadcast(by_head),
+                op=ALU.subtract,
+            )
+        weights = tiles(by_head, "weights")
+        for half in halves:
+            nc.scalar.activation(out=weights[half][:], in_=shifted[half][:], func=ACT.Exp, scale=SOFTMAX_SCALE)
+        total = tiles([P, HALF_HEADS], "total")
+        for half in halves:
+            nc.vector.tensor_reduce(out=total[half][:], in_=weights[half][:], axis=AXIS.X, op=ALU.add)
+        inverse = tiles([P, HALF_HEADS], "inverse")
+        for half in halves:
+            nc.vector.reciprocal(out=inverse[half][:], in_=total[half][:])
+        result = tiles(by_head, "result")
+        for half in halves:
+            nc.vector.tensor_tensor(
+                out=result[half][:],
+                in0=weights[half][:],
+                in1=inverse[half][:].unsqueeze(2).to_broadcast(by_head),
+                op=ALU.mult,
+            )
 
-        half_p = P // CLIPS
-        nc.sync.dma_start(out=out[0].rearrange("h n f g -> (n f) h g"), in_=result[:half_p])
-        nc.scalar.dma_start(out=out[1].rearrange("h n f g -> (n f) h g"), in_=result[half_p:])
+        for half in halves:
+            heads = slice(half * HALF_HEADS, (half + 1) * HALF_HEADS)
+            for b in range(CLIPS):
+                queue = nc.sync if b == 0 else nc.scalar
+                queue.dma_start(
+                    out=out[b, heads].rearrange("h n f g -> (n f) h g"),
+                    in_=result[half][b * (P // CLIPS) : (b + 1) * (P // CLIPS)],
+                )

@@ -51,10 +51,10 @@ def tile_dividedspacetimeattention_pa_s_kernel(tc, x, Wq, bq, k, out):
         load_weights(0)
         x_rows = keep.tile([P, DIM], BF16)
         nc.sync.dma_start(out=x_rows[:], in_=x.rearrange("b t c -> (b t) c"))
-        load_weights(1)
-        bias = keep.tile([P, HEADS, PACK], BF16)
-        nc.sync.dma_start(out=bias[:], in_=bq.rearrange("(h m i) -> m h i", h=HEADS, i=PACK))
-        for h in range(2, HEADS):
+        b_rows = keep.tile([P, FEATURES], BF16)
+        nc.vector.memset(b_rows[:], 0.0)
+        nc.sync.dma_start(out=b_rows[:HEADS], in_=bq.rearrange("(h d) -> h d", h=HEADS))
+        for h in range(1, HEADS):
             load_weights(h)
         k_rows = [keep.tile([P, HEADS // 2, FEATURES], BF16, name="k_rows%d" % b) for b in range(CLIPS)]
         for b in range(CLIPS):
@@ -95,6 +95,17 @@ def tile_dividedspacetimeattention_pa_s_kernel(tc, x, Wq, bq, k, out):
             for b in range(CLIPS):
                 nc.vector.tensor_copy(out=x_grouped_words[:, b], in_=x_t_words[:, b])
             nc.vector.quantize_mx(out=x_codes[:].bitcast(FP8X4), scales=x_scales[:], in_=x_grouped[:])
+
+        bias = keep.tile([P, HEADS, PACK], BF16)
+
+        def spread_bias():
+            b_t = psum_s.tile([P, PAIR, P], F32, tag="s")
+            for u in range(PAIR):
+                transpose_words(b_t[:, u, :], b_rows[:], u)
+            nc.vector.tensor_copy(
+                out=bias[:].rearrange("p h i -> p (h i)").bitcast(F32).rearrange("p (h u) -> p h u", u=PAIR),
+                in_=b_t[:, :, :HEADS].rearrange("p u h -> p h u"),
+            )
 
         w_codes = keep.tile([P, HEADS, FEATURES], U32, align_bytes=64)
         w_scales = keep.tile([P, HEADS, FEATURES], U8, align_bytes=64)
@@ -179,6 +190,7 @@ def tile_dividedspacetimeattention_pa_s_kernel(tc, x, Wq, bq, k, out):
 
         regroup(0)
         quantise_x()
+        spread_bias()
         for r in range(HEADS + 1):
             if r < HEADS:
                 project(r)

@@ -76,6 +76,9 @@ def tile_dividedspacetimeattention_pa_s_kernel(tc, x, Wq, bq, k, out):
             op=ALU.add,
         )
 
+        share = keep.tile([P, 2], F32)
+        nc.vector.tensor_scalar(out=share[:], in0=parity[:], scalar1=-SOFTMAX_SCALE, scalar2=None, op0=ALU.mult)
+
         def transpose_words(dst, rows, u):
             words = rows.bitcast(F32).rearrange("r (p u) -> r p u", u=PAIR)
             nc.tensor.transpose(dst, words[:, :, u], ident[:])
@@ -233,37 +236,33 @@ def tile_dividedspacetimeattention_pa_s_kernel(tc, x, Wq, bq, k, out):
                 leave(out=near[half][rows], in_=s_all[half][rows, :, 2 * c : 2 * c + 2, :])
         second = tiles(by_head, "second")
         for half in halves:
-            nc.vector.tensor_scalar(
-                out=second[half][:], in0=near[half][:, :, 1, :], scalar1=parity[:, 1:2], scalar2=None, op0=ALU.mult
-            )
-        scores = tiles(by_head, "scores")
+            nc.scalar.activation(out=second[half][:], in_=near[half][:, :, 1, :], func=ACT.Copy, scale=share[:, 1:2])
+        lowered = tiles(by_head, "lowered")
         for half in halves:
             nc.vector.scalar_tensor_tensor(
-                out=scores[half][:],
+                out=lowered[half][:],
                 in0=near[half][:, :, 0, :],
-                scalar=parity[:, 0:1],
+                scalar=share[:, 0:1],
                 in1=second[half][:],
                 op0=ALU.mult,
                 op1=ALU.add,
             )
 
-        top = tiles([P, HALF_HEADS], "top")
+        least = tiles([P, HALF_HEADS], "least")
         for half in halves:
-            nc.vector.tensor_reduce(out=top[half][:], in_=scores[half][:], axis=AXIS.X, op=ALU.max)
-        shifted = tiles(by_head, "shifted")
-        for half in halves:
-            nc.vector.tensor_tensor(
-                out=shifted[half][:],
-                in0=scores[half][:],
-                in1=top[half][:].unsqueeze(2).to_broadcast(by_head),
-                op=ALU.subtract,
-            )
+            nc.vector.tensor_reduce(out=least[half][:], in_=lowered[half][:], axis=AXIS.X, op=ALU.min)
         weights = tiles(by_head, "weights")
-        for half in halves:
-            nc.scalar.activation(out=weights[half][:], in_=shifted[half][:], func=ACT.Exp, scale=SOFTMAX_SCALE)
         total = tiles([P, HALF_HEADS], "total")
         for half in halves:
-            nc.vector.tensor_reduce(out=total[half][:], in_=weights[half][:], axis=AXIS.X, op=ALU.add)
+            for hh in range(HALF_HEADS):
+                nc.scalar.activation(
+                    out=weights[half][:, hh, :],
+                    in_=lowered[half][:, hh, :],
+                    func=ACT.Exp,
+                    scale=-1.0,
+                    bias=least[half][:, hh : hh + 1],
+                    accum_out=total[half][:, hh : hh + 1],
+                )
         inverse = tiles([P, HALF_HEADS], "inverse")
         for half in halves:
             nc.vector.reciprocal(out=inverse[half][:], in_=total[half][:])

@@ -24,7 +24,8 @@ GROUPS = CLIPS * PATCHES
 HALF_HEADS = HEADS // 2
 SOFTMAX_SCALE = 1.0 / 64.0
 
-VECTOR_COLUMNS = 40
+VECTOR_COLUMNS = 32
+FIRST_VECTOR_COLUMNS = 40
 KEYS_ROUND = 5
 
 FLOPS = 2 * TOKENS * DIM * HEADS * FEATURES + 2 * GROUPS * HEADS * FRAMES * FRAMES * FEATURES
@@ -116,14 +117,14 @@ def tile_dividedspacetimeattention_pa_s_kernel(tc, x, Wq, bq, k, out):
         q_scales = keep.tile([P, HEADS, TOKENS], U8, align_bytes=64)
         w_grouped, y_t, q_grouped = {}, {}, {}
 
-        def regroup(h):
+        def regroup(h, vector_columns):
             w_grouped[h] = stage.tile(
                 [P, FEATURES * PACK], BF16, align_bytes=64, tag="w_grouped", name="w_grouped%d" % h
             )
             dst = w_grouped[h][:].rearrange("p (i m j) -> p m j i", i=PACK, j=PACK)
             src = w_rows[h][:].rearrange("p j (m i) -> p m j i", i=PACK)
-            nc.vector.tensor_copy(out=dst[:, :VECTOR_COLUMNS], in_=src[:, :VECTOR_COLUMNS])
-            nc.scalar.copy(out=dst[:, VECTOR_COLUMNS:], in_=src[:, VECTOR_COLUMNS:])
+            nc.vector.tensor_copy(out=dst[:, :vector_columns], in_=src[:, :vector_columns])
+            nc.scalar.copy(out=dst[:, vector_columns:], in_=src[:, vector_columns:])
 
         def project(h):
             nc.vector.quantize_mx(
@@ -191,7 +192,7 @@ def tile_dividedspacetimeattention_pa_s_kernel(tc, x, Wq, bq, k, out):
                 in_=k_grouped[:, half * columns : (half + 1) * columns],
             )
 
-        regroup(0)
+        regroup(0, FIRST_VECTOR_COLUMNS)
         quantise_x()
         spread_bias()
         for r in range(HEADS + 1):
@@ -200,7 +201,7 @@ def tile_dividedspacetimeattention_pa_s_kernel(tc, x, Wq, bq, k, out):
             if r >= 1:
                 add_bias(r - 1)
             if r + 1 < HEADS:
-                regroup(r + 1)
+                regroup(r + 1, VECTOR_COLUMNS)
             else:
                 quantise_keys(r + 1 - HEADS)
             if r >= 1:

@@ -69,16 +69,6 @@ def tile_dividedspacetimeattention_pa_s_kernel(tc, x, Wq, bq, k, out):
 
         ident = keep.tile([P, P], F32)
         make_identity(nc, ident[:])
-        parity = keep.tile([P, 2], F32)
-        nc.vector.tensor_reduce(
-            out=parity[:],
-            in_=ident[:].rearrange("p (q e f) -> p e q f", e=2, f=FRAMES),
-            axis=AXIS.XY,
-            op=ALU.add,
-        )
-
-        share = keep.tile([P, 2], F32)
-        nc.vector.tensor_scalar(out=share[:], in0=parity[:], scalar1=-SOFTMAX_SCALE, scalar2=None, op0=ALU.mult)
 
         def transpose_words(dst, rows, u):
             words = rows.bitcast(F32).rearrange("r (p u) -> r p u", u=PAIR)
@@ -92,12 +82,12 @@ def tile_dividedspacetimeattention_pa_s_kernel(tc, x, Wq, bq, k, out):
             for u in range(PAIR):
                 transpose_words(x_t[:, u, :], x_rows[:], u)
             x_grouped = keep.tile([P, TOKENS * PACK], BF16, align_bytes=64)
-            x_grouped_words = x_grouped[:].bitcast(F32).rearrange(
-                "p (b n f u) -> p b n f u", b=CLIPS, n=PATCHES, f=FRAMES
+            nc.vector.tensor_copy(
+                out=x_grouped[:].bitcast(F32).rearrange(
+                    "p (n f b u) -> p n f b u", n=PATCHES, f=FRAMES, b=CLIPS
+                ),
+                in_=x_t[:].rearrange("p u (b f n) -> p n f b u", b=CLIPS, f=FRAMES),
             )
-            x_t_words = x_t[:].rearrange("p u (b f n) -> p b n f u", b=CLIPS, f=FRAMES)
-            for b in range(CLIPS):
-                nc.vector.tensor_copy(out=x_grouped_words[:, b], in_=x_t_words[:, b])
             nc.vector.quantize_mx(out=x_codes[:].bitcast(FP8X4), scales=x_scales[:], in_=x_grouped[:])
 
         bias = keep.tile([P, HEADS, PACK], BF16)
@@ -163,7 +153,7 @@ def tile_dividedspacetimeattention_pa_s_kernel(tc, x, Wq, bq, k, out):
 
         k_grouped = keep.tile([P, HEADS * TOKENS * PACK], BF16, align_bytes=64)
         k_grouped_words = k_grouped[:].bitcast(F32).rearrange(
-            "p (h b c u) -> p h b c u", h=HEADS, b=CLIPS, u=PAIR
+            "p (h n b g u) -> p h n b g u", h=HEADS, n=PATCHES, b=CLIPS, u=PAIR
         )
         k_codes = keep.tile([P, HEADS, TOKENS], U32, align_bytes=64)
         k_scales = keep.tile([P, HEADS, TOKENS], U8, align_bytes=64)
@@ -182,8 +172,8 @@ def tile_dividedspacetimeattention_pa_s_kernel(tc, x, Wq, bq, k, out):
             heads = slice(half * HALF_HEADS, (half + 1) * HALF_HEADS)
             for b in range(CLIPS):
                 nc.scalar.copy(
-                    out=k_grouped_words[:, heads, b],
-                    in_=k_t[half, b][:].rearrange("p u (h c) -> p h c u", h=HALF_HEADS),
+                    out=k_grouped_words[:, heads, :, b],
+                    in_=k_t[half, b][:].rearrange("p u (h n g) -> p h n g u", h=HALF_HEADS, n=PATCHES),
                 )
             columns = HALF_HEADS * TOKENS * PACK
             nc.vector.quantize_mx(
@@ -191,6 +181,81 @@ def tile_dividedspacetimeattention_pa_s_kernel(tc, x, Wq, bq, k, out):
                 scales=k_scales[:, heads, :].rearrange("p h c -> p (h c)"),
                 in_=k_grouped[:, half * columns : (half + 1) * columns],
             )
+
+        PARTS = (slice(0, 4), slice(4, 6), slice(6, 8))
+        parts = range(len(PARTS))
+        counts = [(part.stop - part.start) * CLIPS for part in PARTS]
+
+        def tiles(name, frames):
+            return [keep.tile([P, counts[i], frames], F32, name="%s%d" % (name, i)) for i in parts]
+
+        lowered = tiles("lowered", FRAMES)
+        least = tiles("least", 1)
+        weights = tiles("weights", FRAMES)
+        total = tiles("total", 1)
+        inverse = tiles("inverse", 1)
+        result = tiles("result", FRAMES)
+        s_all = {}
+
+        def score(i):
+            pool, tag = (psum_k, "k_t") if i == 2 else (psum_s, "s")
+            s_all[i] = pool.tile([P, counts[i] // CLIPS, PATCHES, CLIPS, FRAMES], F32, tag=tag, name="s_all%d" % i)
+            for hh, h in enumerate(range(PARTS[i].start, PARTS[i].stop)):
+                nc.tensor.matmul_mx(
+                    out=s_all[i][:, hh].rearrange("p n b g -> p (n b g)"),
+                    lhsT=q_codes[:, h, :].bitcast(FP8X4),
+                    lhsT_scale=q_scales[:, h, :],
+                    rhs=k_codes[:, h, :].bitcast(FP8X4),
+                    rhs_scale=k_scales[:, h, :],
+                    start=True,
+                    stop=True,
+                )
+
+        def leave_psum(i, on_scalar):
+            for n in range(PATCHES):
+                rows = slice(n * QUADRANT, (n + 1) * QUADRANT)
+                to = lowered[i][rows].rearrange("p (h b) g -> p h b g", b=CLIPS)
+                if on_scalar:
+                    nc.scalar.activation(out=to, in_=s_all[i][rows, :, n], func=ACT.Copy, scale=-SOFTMAX_SCALE)
+                else:
+                    nc.vector.tensor_scalar(
+                        out=to, in0=s_all[i][rows, :, n], scalar1=-SOFTMAX_SCALE, scalar2=None, op0=ALU.mult
+                    )
+
+        def find_least(i):
+            nc.vector.tensor_reduce(
+                out=least[i][:].rearrange("p j o -> p (j o)"), in_=lowered[i][:], axis=AXIS.X, op=ALU.min
+            )
+
+        def exponentiate(i):
+            for j in range(counts[i]):
+                nc.scalar.activation(
+                    out=weights[i][:, j, :],
+                    in_=lowered[i][:, j, :],
+                    func=ACT.Exp,
+                    scale=-1.0,
+                    bias=least[i][:, j, :],
+                    accum_out=total[i][:, j, :],
+                )
+
+        def invert(i):
+            nc.vector.reciprocal(out=inverse[i][:], in_=total[i][:])
+
+        def normalise(i):
+            nc.vector.tensor_tensor(
+                out=result[i][:],
+                in0=weights[i][:],
+                in1=inverse[i][:].to_broadcast([P, counts[i], FRAMES]),
+                op=ALU.mult,
+            )
+
+        def store(i):
+            for b in range(CLIPS):
+                queue = nc.sync if b == 0 else nc.scalar
+                queue.dma_start(
+                    out=out[b, PARTS[i]].rearrange("h n f g -> (n f) h g"),
+                    in_=result[i][b:P:CLIPS].rearrange("p (h c) g -> p h c g", c=CLIPS)[:, :, b, :],
+                )
 
         regroup(0, FIRST_VECTOR_COLUMNS)
         quantise_x()
@@ -204,83 +269,30 @@ def tile_dividedspacetimeattention_pa_s_kernel(tc, x, Wq, bq, k, out):
                 regroup(r + 1, VECTOR_COLUMNS)
             else:
                 quantise_keys(r + 1 - HEADS)
+            if r == HEADS:
+                score(0)
+                leave_psum(0, True)
             if r >= 1:
                 quantise_q(r - 1)
             if 0 <= r - KEYS_ROUND < 2:
                 transpose_keys(r - KEYS_ROUND)
 
-        s_all = []
-        for half in range(2):
-            s_all.append(psum_s.tile([P, HALF_HEADS, GROUPS, FRAMES], F32, tag="s", name="s_all%d" % half))
-            for hh in range(HALF_HEADS):
-                h = half * HALF_HEADS + hh
-                nc.tensor.matmul_mx(
-                    out=s_all[half][:, hh].rearrange("p j g -> p (j g)"),
-                    lhsT=q_codes[:, h, :].bitcast(FP8X4),
-                    lhsT_scale=q_scales[:, h, :],
-                    rhs=k_codes[:, h, :].bitcast(FP8X4),
-                    rhs_scale=k_scales[:, h, :],
-                    start=True,
-                    stop=True,
-                )
-        halves = range(2)
-        by_head = [P, HALF_HEADS, FRAMES]
-
-        def tiles(shape, name):
-            return [keep.tile(shape, F32, name="%s%d" % (name, half)) for half in halves]
-
-        near = tiles([P, HALF_HEADS, 2, FRAMES], "near")
-        for half in halves:
-            for c in range(P // QUADRANT):
-                rows = slice(c * QUADRANT, (c + 1) * QUADRANT)
-                leave = nc.scalar.copy if c < 2 else nc.vector.tensor_copy
-                leave(out=near[half][rows], in_=s_all[half][rows, :, 2 * c : 2 * c + 2, :])
-        second = tiles(by_head, "second")
-        for half in halves:
-            nc.scalar.activation(out=second[half][:], in_=near[half][:, :, 1, :], func=ACT.Copy, scale=share[:, 1:2])
-        lowered = tiles(by_head, "lowered")
-        for half in halves:
-            nc.vector.scalar_tensor_tensor(
-                out=lowered[half][:],
-                in0=near[half][:, :, 0, :],
-                scalar=share[:, 0:1],
-                in1=second[half][:],
-                op0=ALU.mult,
-                op1=ALU.add,
-            )
-
-        least = tiles([P, HALF_HEADS], "least")
-        for half in halves:
-            nc.vector.tensor_reduce(out=least[half][:], in_=lowered[half][:], axis=AXIS.X, op=ALU.min)
-        weights = tiles(by_head, "weights")
-        total = tiles([P, HALF_HEADS], "total")
-        for half in halves:
-            for hh in range(HALF_HEADS):
-                nc.scalar.activation(
-                    out=weights[half][:, hh, :],
-                    in_=lowered[half][:, hh, :],
-                    func=ACT.Exp,
-                    scale=-1.0,
-                    bias=least[half][:, hh : hh + 1],
-                    accum_out=total[half][:, hh : hh + 1],
-                )
-        inverse = tiles([P, HALF_HEADS], "inverse")
-        for half in halves:
-            nc.vector.reciprocal(out=inverse[half][:], in_=total[half][:])
-        result = tiles(by_head, "result")
-        for half in halves:
-            nc.vector.tensor_tensor(
-                out=result[half][:],
-                in0=weights[half][:],
-                in1=inverse[half][:].unsqueeze(2).to_broadcast(by_head),
-                op=ALU.mult,
-            )
-
-        for half in halves:
-            heads = slice(half * HALF_HEADS, (half + 1) * HALF_HEADS)
-            for b in range(CLIPS):
-                queue = nc.sync if b == 0 else nc.scalar
-                queue.dma_start(
-                    out=out[b, heads].rearrange("h n f g -> (n f) h g"),
-                    in_=result[half][b * (P // CLIPS) : (b + 1) * (P // CLIPS)],
-                )
+        score(1)
+        score(2)
+        leave_psum(1, True)
+        find_least(0)
+        leave_psum(2, False)
+        find_least(1)
+        find_least(2)
+        exponentiate(0)
+        exponentiate(2)
+        exponentiate(1)
+        invert(0)
+        normalise(0)
+        store(0)
+        invert(2)
+        invert(1)
+        normalise(2)
+        normalise(1)
+        store(2)
+        store(1)

@@ -24,8 +24,7 @@ GROUPS = CLIPS * PATCHES
 HALF_HEADS = HEADS // 2
 SOFTMAX_SCALE = 1.0 / 64.0
 
-VECTOR_COLUMNS = 32
-FIRST_VECTOR_COLUMNS = 40
+VECTOR_COLUMNS = (80, 64, 40, 24, 16, 16, 16, 16)
 KEYS_ROUND = 5
 
 FLOPS = 2 * TOKENS * DIM * HEADS * FEATURES + 2 * GROUPS * HEADS * FRAMES * FRAMES * FEATURES
@@ -57,11 +56,16 @@ def tile_dividedspacetimeattention_pa_s_kernel(tc, x, Wq, bq, k, out):
         nc.sync.dma_start(out=b_rows[:HEADS], in_=bq.rearrange("(h d) -> h d", h=HEADS))
         for h in range(1, HEADS):
             load_weights(h)
-        k_rows = [keep.tile([P, HEADS // 2, FEATURES], BF16, name="k_rows%d" % b) for b in range(CLIPS)]
-        for b in range(CLIPS):
-            nc.sync.dma_start(
-                out=k_rows[b][:], in_=k[b].rearrange("h n g d -> (h n g) d").rearrange("(s p) d -> p s d", p=P)
-            )
+        k_rows = {}
+        for half in range(2):
+            for b in range(CLIPS):
+                k_rows[half, b] = keep.tile([P, HALF_HEADS // 2, FEATURES], BF16, name="k_rows%d%d" % (half, b))
+                nc.sync.dma_start(
+                    out=k_rows[half, b][:],
+                    in_=k[b, half * HALF_HEADS : (half + 1) * HALF_HEADS]
+                    .rearrange("h n g d -> (h n g) d")
+                    .rearrange("(s p) d -> p s d", p=P),
+                )
 
         warm = keep.tile([P, 1], F32)
         nc.vector.memset(warm[:], 0.0)
@@ -77,17 +81,20 @@ def tile_dividedspacetimeattention_pa_s_kernel(tc, x, Wq, bq, k, out):
         x_codes = keep.tile([P, TOKENS], U32, align_bytes=64)
         x_scales = keep.tile([P, TOKENS], U8, align_bytes=64)
 
-        def quantise_x():
+        x_grouped = keep.tile([P, TOKENS * PACK], BF16, align_bytes=64)
+
+        def transpose_x():
             x_t = psum_s.tile([P, PAIR, TOKENS], F32, tag="s")
             for u in range(PAIR):
                 transpose_words(x_t[:, u, :], x_rows[:], u)
-            x_grouped = keep.tile([P, TOKENS * PACK], BF16, align_bytes=64)
-            nc.vector.tensor_copy(
+            nc.scalar.copy(
                 out=x_grouped[:].bitcast(F32).rearrange(
                     "p (n f b u) -> p n f b u", n=PATCHES, f=FRAMES, b=CLIPS
                 ),
                 in_=x_t[:].rearrange("p u (b f n) -> p n f b u", b=CLIPS, f=FRAMES),
             )
+
+        def quantise_x():
             nc.vector.quantize_mx(out=x_codes[:].bitcast(FP8X4), scales=x_scales[:], in_=x_grouped[:])
 
         bias = keep.tile([P, HEADS, PACK], BF16)
@@ -96,7 +103,7 @@ def tile_dividedspacetimeattention_pa_s_kernel(tc, x, Wq, bq, k, out):
             b_t = psum_s.tile([P, PAIR, P], F32, tag="s")
             for u in range(PAIR):
                 transpose_words(b_t[:, u, :], b_rows[:], u)
-            nc.vector.tensor_copy(
+            nc.scalar.copy(
                 out=bias[:].rearrange("p h i -> p (h i)").bitcast(F32).rearrange("p (h u) -> p h u", u=PAIR),
                 in_=b_t[:, :, :HEADS].rearrange("p u h -> p h u"),
             )
@@ -107,7 +114,8 @@ def tile_dividedspacetimeattention_pa_s_kernel(tc, x, Wq, bq, k, out):
         q_scales = keep.tile([P, HEADS, TOKENS], U8, align_bytes=64)
         w_grouped, y_t, q_grouped = {}, {}, {}
 
-        def regroup(h, vector_columns):
+        def regroup(h):
+            vector_columns = VECTOR_COLUMNS[h]
             w_grouped[h] = stage.tile(
                 [P, FEATURES * PACK], BF16, align_bytes=64, tag="w_grouped", name="w_grouped%d" % h
             )
@@ -116,10 +124,12 @@ def tile_dividedspacetimeattention_pa_s_kernel(tc, x, Wq, bq, k, out):
             nc.vector.tensor_copy(out=dst[:, :vector_columns], in_=src[:, :vector_columns])
             nc.scalar.copy(out=dst[:, vector_columns:], in_=src[:, vector_columns:])
 
-        def project(h):
+        def quantise_w(h):
             nc.vector.quantize_mx(
                 out=w_codes[:, h, :].bitcast(FP8X4), scales=w_scales[:, h, :], in_=w_grouped[h][:]
             )
+
+        def project(h):
             y_t[h] = psum_y.tile([P, PACK, TOKENS], F32, tag="y_t", name="y_t%d" % h)
             for i in range(PACK):
                 quarter = slice(i * P, (i + 1) * P)
@@ -159,13 +169,13 @@ def tile_dividedspacetimeattention_pa_s_kernel(tc, x, Wq, bq, k, out):
         k_scales = keep.tile([P, HEADS, TOKENS], U8, align_bytes=64)
         k_t = {}
 
-        def transpose_keys(b):
-            for half in range(2):
+        def transpose_keys(half):
+            for b in range(CLIPS):
                 k_t[half, b] = psum_k.tile([P, PAIR, 2 * P], F32, tag="k_t", name="k_t%d%d" % (half, b))
                 for s in range(2):
                     for u in range(PAIR):
                         transpose_words(
-                            k_t[half, b][:, u, s * P : (s + 1) * P], k_rows[b][:, half * 2 + s, :], u
+                            k_t[half, b][:, u, s * P : (s + 1) * P], k_rows[half, b][:, s, :], u
                         )
 
         def quantise_keys(half):
@@ -257,23 +267,26 @@ def tile_dividedspacetimeattention_pa_s_kernel(tc, x, Wq, bq, k, out):
                     in_=result[i][b:P:CLIPS].rearrange("p (h c) g -> p h c g", c=CLIPS)[:, :, b, :],
                 )
 
-        regroup(0, FIRST_VECTOR_COLUMNS)
-        quantise_x()
+        regroup(0)
+        transpose_x()
         spread_bias()
-        for r in range(HEADS + 1):
+        quantise_w(0)
+        quantise_x()
+        project(0)
+        regroup(1)
+        for r in range(1, HEADS + 1):
             if r < HEADS:
+                quantise_w(r)
                 project(r)
-            if r >= 1:
-                add_bias(r - 1)
+            add_bias(r - 1)
             if r + 1 < HEADS:
-                regroup(r + 1, VECTOR_COLUMNS)
+                regroup(r + 1)
             else:
                 quantise_keys(r + 1 - HEADS)
             if r == HEADS:
                 score(0)
                 leave_psum(0, True)
-            if r >= 1:
-                quantise_q(r - 1)
+            quantise_q(r - 1)
             if 0 <= r - KEYS_ROUND < 2:
                 transpose_keys(r - KEYS_ROUND)
 

@@ -24,7 +24,7 @@ GROUPS = CLIPS * PATCHES
 HALF_HEADS = HEADS // 2
 SOFTMAX_SCALE = 1.0 / 64.0
 
-VECTOR_COLUMNS = (80, 64, 40, 24, 16, 16, 16, 16)
+VECTOR_COLUMNS = (88, 72, 48, 40, 32, 24, 24, 16)
 KEYS_ROUND = 5
 
 FLOPS = 2 * TOKENS * DIM * HEADS * FEATURES + 2 * GROUPS * HEADS * FRAMES * FRAMES * FEATURES

@@ -74,6 +74,9 @@ def tile_dividedspacetimeattention_pa_s_kernel(tc, x, Wq, bq, k, out):
         ident = keep.tile([P, P], F32)
         make_identity(nc, ident[:])
 
+        def transpose_pairs(dst, rows, u):
+            nc.tensor.transpose(dst, rows.bitcast(F32)[:, u * P : (u + 1) * P], ident[:])
+
         def transpose_words(dst, rows, u):
             words = rows.bitcast(F32).rearrange("r (p u) -> r p u", u=PAIR)
             nc.tensor.transpose(dst, words[:, :, u], ident[:])
@@ -102,7 +105,7 @@ def tile_dividedspacetimeattention_pa_s_kernel(tc, x, Wq, bq, k, out):
         def spread_bias():
             b_t = psum_s.tile([P, PAIR, P], F32, tag="s")
             for u in range(PAIR):
-                transpose_words(b_t[:, u, :], b_rows[:], u)
+                transpose_pairs(b_t[:, u, :], b_rows[:], u)
             nc.scalar.copy(
                 out=bias[:].rearrange("p h i -> p (h i)").bitcast(F32).rearrange("p (h u) -> p h u", u=PAIR),
                 in_=b_t[:, :, :HEADS].rearrange("p u h -> p h u"),
@@ -119,8 +122,8 @@ def tile_dividedspacetimeattention_pa_s_kernel(tc, x, Wq, bq, k, out):
             w_grouped[h] = stage.tile(
                 [P, FEATURES * PACK], BF16, align_bytes=64, tag="w_grouped", name="w_grouped%d" % h
             )
-            dst = w_grouped[h][:].rearrange("p (i m j) -> p m j i", i=PACK, j=PACK)
-            src = w_rows[h][:].rearrange("p j (m i) -> p m j i", i=PACK)
+            dst = w_grouped[h][:].rearrange("p (e k v j) -> p k j v e", e=PAIR, v=2, j=PACK)
+            src = w_rows[h][:].rearrange("p j (k v e) -> p k j v e", v=2, e=PAIR)
             nc.vector.tensor_copy(out=dst[:, :vector_columns], in_=src[:, :vector_columns])
             nc.scalar.copy(out=dst[:, vector_columns:], in_=src[:, vector_columns:])
 
@@ -148,9 +151,9 @@ def tile_dividedspacetimeattention_pa_s_kernel(tc, x, Wq, bq, k, out):
                 [P, TOKENS, PACK], BF16, align_bytes=64, tag="q_grouped", name="q_grouped%d" % h
             )
             nc.vector.tensor_tensor(
-                out=q_grouped[h][:],
-                in0=y_t[h][:].rearrange("p i t -> p t i"),
-                in1=bias[:, h, :].unsqueeze(1).to_broadcast([P, TOKENS, PACK]),
+                out=q_grouped[h][:].rearrange("p t (u e) -> p t u e", u=PAIR),
+                in0=y_t[h][:].rearrange("p (e u) t -> p t u e", e=PAIR),
+                in1=bias[:, h, :].rearrange("p (u e) -> p u e", u=PAIR).unsqueeze(1).to_broadcast([P, TOKENS, PAIR, PAIR]),
                 op=ALU.add,
             )
 
@@ -174,7 +177,7 @@ def tile_dividedspacetimeattention_pa_s_kernel(tc, x, Wq, bq, k, out):
                 k_t[half, b] = psum_k.tile([P, PAIR, 2 * P], F32, tag="k_t", name="k_t%d%d" % (half, b))
                 for s in range(2):
                     for u in range(PAIR):
-                        transpose_words(
+                        transpose_pairs(
                             k_t[half, b][:, u, s * P : (s + 1) * P], k_rows[half, b][:, s, :], u
                         )
 

from contextlib import ExitStack

import concourse.mybir as mybir
from concourse.masks import make_identity

FP8X4 = mybir.dt.float8_e4m3fn_x4
BF16 = mybir.dt.bfloat16
F32 = mybir.dt.float32
U32 = mybir.dt.uint32
U8 = mybir.dt.uint8
ALU = mybir.AluOpType
ACT = mybir.ActivationFunctionType
AXIS = mybir.AxisListType

P = 128
QUADRANT = 32
PACK = 4
PAIR = 2
CLIPS, PATCHES, FRAMES, HEADS = 2, 4, 16, 8
DIM = 512
FEATURES = 512
TOKENS = CLIPS * PATCHES * FRAMES
GROUPS = CLIPS * PATCHES
HALF_HEADS = HEADS // 2
SOFTMAX_SCALE = 1.0 / 64.0

VECTOR_COLUMNS = (88, 72, 48, 40, 32, 24, 24, 16)
KEYS_ROUND = 5

FLOPS = 2 * TOKENS * DIM * HEADS * FEATURES + 2 * GROUPS * HEADS * FRAMES * FRAMES * FEATURES


def tile_dividedspacetimeattention_pa_s_kernel(tc, x, Wq, bq, k, out):
    nc = tc.nc
    with ExitStack() as ctx:
        ctx.enter_context(tc.manual_schedule())
        keep = ctx.enter_context(tc.tile_pool(name="keep", bufs=1))
        stage = ctx.enter_context(tc.tile_pool(name="stage", bufs=3))
        psum_y = ctx.enter_context(tc.psum_pool(name="psum_y", bufs=2))
        psum_k = ctx.enter_context(tc.psum_pool(name="psum_k", bufs=4))
        psum_s = ctx.enter_context(tc.psum_pool(name="psum_s", bufs=2))

        w_rows = [keep.tile([P, PACK, FEATURES], BF16, name="w_rows%d" % h) for h in range(HEADS)]

        def load_weights(h):
            nc.sync.dma_start(
                out=w_rows[h][:],
                in_=Wq[:, h * FEATURES : (h + 1) * FEATURES].rearrange("(p j) w -> p j w", j=PACK),
            )

        load_weights(0)
        x_rows = keep.tile([P, DIM], BF16)
        nc.sync.dma_start(out=x_rows[:], in_=x.rearrange("b t c -> (b t) c"))
        b_rows = keep.tile([P, FEATURES], BF16)
        nc.vector.memset(b_rows[:], 0.0)
        nc.sync.dma_start(out=b_rows[:HEADS], in_=bq.rearrange("(h d) -> h d", h=HEADS))
        for h in range(1, HEADS):
            load_weights(h)
        k_rows = {}
        for half in range(2):
            for b in range(CLIPS):
                k_rows[half, b] = keep.tile([P, HALF_HEADS // 2, FEATURES], BF16, name="k_rows%d%d" % (half, b))
                nc.sync.dma_start(
                    out=k_rows[half, b][:],
                    in_=k[b, half * HALF_HEADS : (half + 1) * HALF_HEADS]
                    .rearrange("h n g d -> (h n g) d")
                    .rearrange("(s p) d -> p s d", p=P),
                )

        warm = keep.tile([P, 1], F32)
        nc.vector.memset(warm[:], 0.0)
        nc.scalar.activation(out=warm[:], in_=warm[:], func=ACT.Exp)

        ident = keep.tile([P, P], F32)
        make_identity(nc, ident[:])

        def transpose_pairs(dst, rows, u):
            nc.tensor.transpose(dst, rows.bitcast(F32)[:, u * P : (u + 1) * P], ident[:])

        def transpose_words(dst, rows, u):
            words = rows.bitcast(F32).rearrange("r (p u) -> r p u", u=PAIR)
            nc.tensor.transpose(dst, words[:, :, u], ident[:])

        x_codes = keep.tile([P, TOKENS], U32, align_bytes=64)
        x_scales = keep.tile([P, TOKENS], U8, align_bytes=64)

        x_grouped = keep.tile([P, TOKENS * PACK], BF16, align_bytes=64)

        def transpose_x():
            x_t = psum_s.tile([P, PAIR, TOKENS], F32, tag="s")
            for u in range(PAIR):
                transpose_words(x_t[:, u, :], x_rows[:], u)
            nc.scalar.copy(
                out=x_grouped[:].bitcast(F32).rearrange(
                    "p (n f b u) -> p n f b u", n=PATCHES, f=FRAMES, b=CLIPS
                ),
                in_=x_t[:].rearrange("p u (b f n) -> p n f b u", b=CLIPS, f=FRAMES),
            )

        def quantise_x():
            nc.vector.quantize_mx(out=x_codes[:].bitcast(FP8X4), scales=x_scales[:], in_=x_grouped[:])

        bias = keep.tile([P, HEADS, PACK], BF16)

        def spread_bias():
            b_t = psum_s.tile([P, PAIR, P], F32, tag="s")
            for u in range(PAIR):
                transpose_pairs(b_t[:, u, :], b_rows[:], u)
            nc.scalar.copy(
                out=bias[:].rearrange("p h i -> p (h i)").bitcast(F32).rearrange("p (h u) -> p h u", u=PAIR),
                in_=b_t[:, :, :HEADS].rearrange("p u h -> p h u"),
            )

        w_codes = keep.tile([P, HEADS, FEATURES], U32, align_bytes=64)
        w_scales = keep.tile([P, HEADS, FEATURES], U8, align_bytes=64)
        q_codes = keep.tile([P, HEADS, TOKENS], U32, align_bytes=64)
        q_scales = keep.tile([P, HEADS, TOKENS], U8, align_bytes=64)
        w_grouped, y_t, q_grouped = {}, {}, {}

        def regroup(h):
            vector_columns = VECTOR_COLUMNS[h]
            w_grouped[h] = stage.tile(
                [P, FEATURES * PACK], BF16, align_bytes=64, tag="w_grouped", name="w_grouped%d" % h
            )
            dst = w_grouped[h][:].rearrange("p (e k v j) -> p k j v e", e=PAIR, v=2, j=PACK)
            src = w_rows[h][:].rearrange("p j (k v e) -> p k j v e", v=2, e=PAIR)
            nc.vector.tensor_copy(out=dst[:, :vector_columns], in_=src[:, :vector_columns])
            nc.scalar.copy(out=dst[:, vector_columns:], in_=src[:, vector_columns:])

        def quantise_w(h):
            nc.vector.quantize_mx(
                out=w_codes[:, h, :].bitcast(FP8X4), scales=w_scales[:, h, :], in_=w_grouped[h][:]
            )

        def project(h):
            y_t[h] = psum_y.tile([P, PACK, TOKENS], F32, tag="y_t", name="y_t%d" % h)
            for i in range(PACK):
                quarter = slice(i * P, (i + 1) * P)
                nc.tensor.matmul_mx(
                    out=y_t[h][:, i, :],
                    lhsT=w_codes[:, h, quarter].bitcast(FP8X4),
                    lhsT_scale=w_scales[:, h, quarter],
                    rhs=x_codes[:].bitcast(FP8X4),
                    rhs_scale=x_scales[:],
                    start=True,
                    stop=True,
                )

        def add_bias(h):
            q_grouped[h] = stage.tile(
                [P, TOKENS, PACK], BF16, align_bytes=64, tag="q_grouped", name="q_grouped%d" % h
            )
            nc.vector.tensor_tensor(
                out=q_grouped[h][:].rearrange("p t (u e) -> p t u e", u=PAIR),
                in0=y_t[h][:].rearrange("p (e u) t -> p t u e", e=PAIR),
                in1=bias[:, h, :].rearrange("p (u e) -> p u e", u=PAIR).unsqueeze(1).to_broadcast([P, TOKENS, PAIR, PAIR]),
                op=ALU.add,
            )

        def quantise_q(h):
            nc.vector.quantize_mx(
                out=q_codes[:, h, :].bitcast(FP8X4),
                scales=q_scales[:, h, :],
                in_=q_grouped[h][:].rearrange("p t i -> p (t i)"),
            )

        k_grouped = keep.tile([P, HEADS * TOKENS * PACK], BF16, align_bytes=64)
        k_grouped_words = k_grouped[:].bitcast(F32).rearrange(
            "p (h n b g u) -> p h n b g u", h=HEADS, n=PATCHES, b=CLIPS, u=PAIR
        )
        k_codes = keep.tile([P, HEADS, TOKENS], U32, align_bytes=64)
        k_scales = keep.tile([P, HEADS, TOKENS], U8, align_bytes=64)
        k_t = {}

        def transpose_keys(half):
            for b in range(CLIPS):
                k_t[half, b] = psum_k.tile([P, PAIR, 2 * P], F32, tag="k_t", name="k_t%d%d" % (half, b))
                for s in range(2):
                    for u in range(PAIR):
                        transpose_pairs(
                            k_t[half, b][:, u, s * P : (s + 1) * P], k_rows[half, b][:, s, :], u
                        )

        def quantise_keys(half):
            heads = slice(half * HALF_HEADS, (half + 1) * HALF_HEADS)
            for b in range(CLIPS):
                nc.scalar.copy(
                    out=k_grouped_words[:, heads, :, b],
                    in_=k_t[half, b][:].rearrange("p u (h n g) -> p h n g u", h=HALF_HEADS, n=PATCHES),
                )
            columns = HALF_HEADS * TOKENS * PACK
            nc.vector.quantize_mx(
                out=k_codes[:, heads, :].rearrange("p h c -> p (h c)").bitcast(FP8X4),
                scales=k_scales[:, heads, :].rearrange("p h c -> p (h c)"),
                in_=k_grouped[:, half * columns : (half + 1) * columns],
            )

        PARTS = (slice(0, 4), slice(4, 6), slice(6, 8))
        parts = range(len(PARTS))
        counts = [(part.stop - part.start) * CLIPS for part in PARTS]

        def tiles(name, frames):
            return [keep.tile([P, counts[i], frames], F32, name="%s%d" % (name, i)) for i in parts]

        lowered = tiles("lowered", FRAMES)
        least = tiles("least", 1)
        weights = tiles("weights", FRAMES)
        total = tiles("total", 1)
        inverse = tiles("inverse", 1)
        result = tiles("result", FRAMES)
        s_all = {}

        def score(i):
            pool, tag = (psum_k, "k_t") if i == 2 else (psum_s, "s")
            s_all[i] = pool.tile([P, counts[i] // CLIPS, PATCHES, CLIPS, FRAMES], F32, tag=tag, name="s_all%d" % i)
            for hh, h in enumerate(range(PARTS[i].start, PARTS[i].stop)):
                nc.tensor.matmul_mx(
                    out=s_all[i][:, hh].rearrange("p n b g -> p (n b g)"),
                    lhsT=q_codes[:, h, :].bitcast(FP8X4),
                    lhsT_scale=q_scales[:, h, :],
                    rhs=k_codes[:, h, :].bitcast(FP8X4),
                    rhs_scale=k_scales[:, h, :],
                    start=True,
                    stop=True,
                )

        def leave_psum(i, on_scalar):
            for n in range(PATCHES):
                rows = slice(n * QUADRANT, (n + 1) * QUADRANT)
                to = lowered[i][rows].rearrange("p (h b) g -> p h b g", b=CLIPS)
                if on_scalar:
                    nc.scalar.activation(out=to, in_=s_all[i][rows, :, n], func=ACT.Copy, scale=-SOFTMAX_SCALE)
                else:
                    nc.vector.tensor_scalar(
                        out=to, in0=s_all[i][rows, :, n], scalar1=-SOFTMAX_SCALE, scalar2=None, op0=ALU.mult
                    )

        def find_least(i):
            nc.vector.tensor_reduce(
                out=least[i][:].rearrange("p j o -> p (j o)"), in_=lowered[i][:], axis=AXIS.X, op=ALU.min
            )

        def exponentiate(i):
            for j in range(counts[i]):
                nc.scalar.activation(
                    out=weights[i][:, j, :],
                    in_=lowered[i][:, j, :],
                    func=ACT.Exp,
                    scale=-1.0,
                    bias=least[i][:, j, :],
                    accum_out=total[i][:, j, :],
                )

        def invert(i):
            nc.vector.reciprocal(out=inverse[i][:], in_=total[i][:])

        def normalise(i):
            nc.vector.tensor_tensor(
                out=result[i][:],
                in0=weights[i][:],
                in1=inverse[i][:].to_broadcast([P, counts[i], FRAMES]),
                op=ALU.mult,
            )

        def store(i):
            for b in range(CLIPS):
                queue = nc.sync if b == 0 else nc.scalar
                queue.dma_start(
                    out=out[b, PARTS[i]].rearrange("h n f g -> (n f) h g"),
                    in_=result[i][b:P:CLIPS].rearrange("p (h c) g -> p h c g", c=CLIPS)[:, :, b, :],
                )

        regroup(0)
        transpose_x()
        spread_bias()
        quantise_w(0)
        quantise_x()
        project(0)
        regroup(1)
        for r in range(1, HEADS + 1):
            if r < HEADS:
                quantise_w(r)
                project(r)
            add_bias(r - 1)
            if r + 1 < HEADS:
                regroup(r + 1)
            else:
                quantise_keys(r + 1 - HEADS)
            if r == HEADS:
                score(0)
                leave_psum(0, True)
            quantise_q(r - 1)
            if 0 <= r - KEYS_ROUND < 2:
                transpose_keys(r - KEYS_ROUND)

        score(1)
        score(2)
        leave_psum(1, True)
        find_least(0)
        leave_psum(2, False)
        find_least(1)
        find_least(2)
        exponentiate(0)
        exponentiate(2)
        exponentiate(1)
        invert(0)
        normalise(0)
        store(0)
        invert(2)
        invert(1)
        normalise(2)
        normalise(1)
        store(2)
        store(1)
